import numpy as np
import ml_dtypes

BF16 = ml_dtypes.bfloat16


def bf(x):
    return np.asarray(x, np.float32).astype(BF16)


def f32(x):
    return np.asarray(x, np.float32)


def f64(x):
    return np.asarray(x).astype(np.float64)


def striped(idx):
    return np.tile(idx.reshape(-1, 16).T, (8, 1))


B, S, N = 512, 1024, 512
THRESHOLD = 0.5
TEMPERATURE = 4.0
LO, HI = 0.3, 0.7


def setup_inputs():
    return {
        "label": f32(np.random.uniform(0.0, 1.0, (B, S))),
        "prob": f32(np.random.uniform(LO, HI, (B, N))),
        "prob_cons": f32(np.random.uniform(LO, HI, (B, N))),
        "row_mask": f32(np.random.uniform(0.0, 1.0, (B, 1)) < 0.5),
        "offs": striped(np.random.permutation(S)[:N]),
    }


def reference(label, prob, prob_cons, row_mask, offs):
    idx = offs[:16].T.reshape(-1)
    o = f64(prob)
    l1 = np.log(o)
    l0 = np.log(1.0 - o)
    d = l1 - l0
    sharp = np.where(o > THRESHOLD, o + (1.0 - o) / TEMPERATURE, o - o / TEMPERATURE)
    bce = -(f64(label)[:, idx] * d + l0)
    per_elem = bce + (o - sharp) ** 2 + (f64(prob_cons) - sharp) ** 2
    return per_elem * f64(row_mask)

@@ -1,0 +1,73 @@
+import concourse.mybir as mybir
+
+F32 = mybir.dt.float32
+U16 = mybir.dt.uint16
+ALU = mybir.AluOpType
+ACT = mybir.ActivationFunctionType
+P = 128
+
+
+def tile_semiloss_kernel(tc, label, prob, prob_cons, row_mask, offs, out):
+    nc = tc.nc
+    samples, classes = label.shape
+    picked = prob.shape[1]
+    blocks = samples // P
+
+    with (
+        tc.tile_pool(name="held", bufs=1) as held,
+        tc.tile_pool(name="loads", bufs=blocks) as loads,
+        tc.tile_pool(name="work", bufs=blocks) as work,
+    ):
+        offsets = held.tile([P, picked // 16], U16, name="offsets")
+        nc.sync.dma_start(offsets[:], offs)
+        mask = held.tile([P, blocks], F32, name="mask")
+
+        p_tiles, c_tiles, y_tiles = [], [], []
+        for i in range(blocks):
+            rows = slice(i * P, (i + 1) * P)
+            p = loads.tile([P, picked], F32, name="p")
+            c = loads.tile([P, picked], F32, name="c")
+            y = loads.tile([P, classes], F32, name="y")
+            nc.sync.dma_start(p[:], prob[rows, :])
+            nc.sync.dma_start(c[:], prob_cons[rows, :])
+            nc.sync.dma_start(y[:], label[rows, :])
+            if i == 0:
+                with nc.allow_non_contiguous_dma(reason="one mask value to a partition, 512 in all"):
+                    nc.sync.dma_start(mask[:], row_mask.rearrange("(n p) one -> p (n one)", p=P))
+            p_tiles.append(p)
+            c_tiles.append(c)
+            y_tiles.append(y)
+
+        for i in range(blocks):
+            p, c, y = p_tiles[i], c_tiles[i], y_tiles[i]
+
+            log_p = work.tile([P, picked], F32, name="log_p")
+            log_q = work.tile([P, picked], F32, name="log_q")
+            nc.scalar.activation(log_p[:], p[:], ACT.Ln)
+            nc.scalar.activation(log_q[:], p[:], ACT.Ln, bias=1.0, scale=-1.0)
+
+            step = work.tile([P, picked], F32, name="step")
+            nc.vector.scalar_tensor_tensor(step[:], p[:], 0.5, p[:], ALU.is_gt, ALU.subtract)
+            gap = work.tile([P, picked], F32, name="gap")
+            nc.vector.tensor_tensor(gap[:], c[:], p[:], ALU.subtract)
+            cons_err = work.tile([P, picked], F32, name="cons_err")
+            nc.vector.scalar_tensor_tensor(cons_err[:], step[:], -0.25, gap[:], ALU.mult, ALU.add)
+
+            sq_own = work.tile([P, picked], F32, name="sq_own")
+            sq_cons = work.tile([P, picked], F32, name="sq_cons")
+            nc.scalar.activation(sq_own[:], step[:], ACT.Square, scale=0.25)
+            nc.scalar.activation(sq_cons[:], cons_err[:], ACT.Square)
+
+            neg_d = work.tile([P, picked], F32, name="neg_d")
+            nc.vector.tensor_tensor(neg_d[:], log_q[:], log_p[:], ALU.subtract)
+            picked_d = work.tile([P, picked], F32, name="picked_d")
+            nc.vector.tensor_tensor(picked_d[:], y[:].indirect(offsets[:]), neg_d[:], ALU.mult)
+
+            total = work.tile([P, picked], F32, name="total")
+            nc.vector.tensor_tensor(total[:], sq_own[:], sq_cons[:], ALU.add)
+            nc.vector.tensor_tensor(total[:], total[:], log_q[:], ALU.subtract)
+            nc.vector.tensor_tensor(total[:], total[:], picked_d[:], ALU.add)
+
+            masked = work.tile([P, picked], F32, name="masked")
+            nc.scalar.activation(masked[:], total[:], ACT.Copy, scale=mask[:, i : i + 1])
+            nc.scalar.dma_start(out[i * P : (i + 1) * P, :], masked[:])

@@ -1,10 +1,12 @@
 import concourse.mybir as mybir
+from concourse.masks import make_identity
 
 F32 = mybir.dt.float32
 U16 = mybir.dt.uint16
 ALU = mybir.AluOpType
 ACT = mybir.ActivationFunctionType
 P = 128
+BF16 = mybir.dt.bfloat16
 
 
 def tile_semiloss_kernel(tc, label, prob, prob_cons, row_mask, offs, out):
@@ -17,57 +19,86 @@ def tile_semiloss_kernel(tc, label, prob, prob_cons, row_mask, offs, out):
         tc.tile_pool(name="held", bufs=1) as held,
         tc.tile_pool(name="loads", bufs=blocks) as loads,
         tc.tile_pool(name="work", bufs=blocks) as work,
+        tc.psum_pool(name="sums", bufs=blocks) as sums,
+        tc.psum_pool(name="turned", bufs=1) as turned,
     ):
         offsets = held.tile([P, picked // 16], U16, name="offsets")
         nc.sync.dma_start(offsets[:], offs)
-        mask = held.tile([P, blocks], F32, name="mask")
+        mask_row = held.tile([1, samples], F32, name="mask_row")
+        nc.scalar.dma_start(mask_row[:], row_mask.rearrange("b one -> one b"))
 
         p_tiles, c_tiles, y_tiles = [], [], []
         for i in range(blocks):
             rows = slice(i * P, (i + 1) * P)
-            p = loads.tile([P, picked], F32, name="p")
             c = loads.tile([P, picked], F32, name="c")
+            p = loads.tile([P, picked], F32, name="p")
             y = loads.tile([P, classes], F32, name="y")
-            nc.sync.dma_start(p[:], prob[rows, :])
             nc.sync.dma_start(c[:], prob_cons[rows, :])
+            nc.sync.dma_start(p[:], prob[rows, :])
             nc.sync.dma_start(y[:], label[rows, :])
-            if i == 0:
-                with nc.allow_non_contiguous_dma(reason="one mask value to a partition, 512 in all"):
-                    nc.sync.dma_start(mask[:], row_mask.rearrange("(n p) one -> p (n one)", p=P))
-            p_tiles.append(p)
             c_tiles.append(c)
+            p_tiles.append(p)
             y_tiles.append(y)
 
+        identity = held.tile([P, P], F32, name="identity")
+        make_identity(nc, identity[:])
+        one = held.tile([1, 1], F32, name="one")
+        nc.vector.memset(one[:], 1.0)
+
+        mask_psum = turned.tile([P, blocks], F32, name="mask_psum")
+        for i in range(blocks):
+            nc.tensor.matmul(mask_psum[:, i : i + 1], mask_row[:, i * P : (i + 1) * P], one[:], start=True, stop=True)
+        mask = held.tile([P, blocks], F32, name="mask")
+        nc.vector.tensor_copy(mask[:], mask_psum[:])
+
+        plus_mask = held.tile([P, blocks, P], F32, name="plus_mask")
+        minus_mask = held.tile([P, blocks, P], F32, name="minus_mask")
+        plus_mask_bf = held.tile([P, blocks, P], BF16, name="plus_mask_bf")
+
+        def finish(i, picked_d, rest):
+            loss = work.tile([P, picked], F32, name="loss")
+            nc.vector.scalar_tensor_tensor(loss[:], picked_d[:], mask[:, i : i + 1], rest[:], ALU.mult, ALU.add)
+            nc.sync.dma_start(out[i * P : (i + 1) * P, :], loss[:])
+
+        waiting = None
         for i in range(blocks):
             p, c, y = p_tiles[i], c_tiles[i], y_tiles[i]
+
+            c4 = work.tile([P, picked], F32, name="c4")
+            nc.scalar.mul(c4[:], c[:], 4.0)
+            smooth = work.tile([P, picked], F32, name="smooth")
+            nc.vector.scalar_tensor_tensor(smooth[:], p[:], -3.0, c4[:], ALU.mult, ALU.add)
+            cons_err = work.tile([P, picked], F32, name="cons_err")
+            nc.vector.scalar_tensor_tensor(cons_err[:], p[:], 0.5, smooth[:], ALU.is_gt, ALU.subtract)
+
+            if i == 0:
+                for k in range(blocks):
+                    nc.vector.tensor_scalar(plus_mask[:, k, :], identity[:], mask[:, k : k + 1], None, ALU.mult)
+                nc.vector.tensor_scalar(minus_mask[:], plus_mask[:], -1.0, None, ALU.mult)
+                nc.vector.tensor_copy(plus_mask_bf[:], plus_mask[:])
+            else:
+                finish(*waiting)
 
             log_p = work.tile([P, picked], F32, name="log_p")
             log_q = work.tile([P, picked], F32, name="log_q")
             nc.scalar.activation(log_p[:], p[:], ACT.Ln)
             nc.scalar.activation(log_q[:], p[:], ACT.Ln, bias=1.0, scale=-1.0)
 
-            step = work.tile([P, picked], F32, name="step")
-            nc.vector.scalar_tensor_tensor(step[:], p[:], 0.5, p[:], ALU.is_gt, ALU.subtract)
-            gap = work.tile([P, picked], F32, name="gap")
-            nc.vector.tensor_tensor(gap[:], c[:], p[:], ALU.subtract)
-            cons_err = work.tile([P, picked], F32, name="cons_err")
-            nc.vector.scalar_tensor_tensor(cons_err[:], step[:], -0.25, gap[:], ALU.mult, ALU.add)
-
-            sq_own = work.tile([P, picked], F32, name="sq_own")
-            sq_cons = work.tile([P, picked], F32, name="sq_cons")
-            nc.scalar.activation(sq_own[:], step[:], ACT.Square, scale=0.25)
-            nc.scalar.activation(sq_cons[:], cons_err[:], ACT.Square)
-
             neg_d = work.tile([P, picked], F32, name="neg_d")
             nc.vector.tensor_tensor(neg_d[:], log_q[:], log_p[:], ALU.subtract)
             picked_d = work.tile([P, picked], F32, name="picked_d")
             nc.vector.tensor_tensor(picked_d[:], y[:].indirect(offsets[:]), neg_d[:], ALU.mult)
 
-            total = work.tile([P, picked], F32, name="total")
-            nc.vector.tensor_tensor(total[:], sq_own[:], sq_cons[:], ALU.add)
-            nc.vector.tensor_tensor(total[:], total[:], log_q[:], ALU.subtract)
-            nc.vector.tensor_tensor(total[:], total[:], picked_d[:], ALU.add)
+            sq_cons = work.tile([P, picked], F32, name="sq_cons")
+            nc.scalar.activation(sq_cons[:], cons_err[:], ACT.Square, scale=0.25)
+            dist = work.tile([P, picked], F32, name="dist")
+            nc.scalar.activation(dist[:], p[:], ACT.Abs, bias=-0.5)
+            sq_own = work.tile([P, picked], BF16, name="sq_own")
+            nc.scalar.activation(sq_own[:], dist[:], ACT.Square, bias=0.125, scale=-0.25)
 
-            masked = work.tile([P, picked], F32, name="masked")
-            nc.scalar.activation(masked[:], total[:], ACT.Copy, scale=mask[:, i : i + 1])
-            nc.scalar.dma_start(out[i * P : (i + 1) * P, :], masked[:])
+            rest = sums.tile([P, picked], F32, name="rest")
+            nc.tensor.matmul(rest[:], minus_mask[:, i, :], log_q[:], start=True, stop=False)
+            nc.tensor.matmul(rest[:], plus_mask[:, i, :], sq_cons[:], start=False, stop=False)
+            nc.tensor.matmul(rest[:], plus_mask_bf[:, i, :], sq_own[:], start=False, stop=True)
+            waiting = (i, picked_d, rest)
+        finish(*waiting)

@@ -20,85 +20,69 @@ def tile_semiloss_kernel(tc, label, prob, prob_cons, row_mask, offs, out):
         tc.tile_pool(name="loads", bufs=blocks) as loads,
         tc.tile_pool(name="work", bufs=blocks) as work,
         tc.psum_pool(name="sums", bufs=blocks) as sums,
-        tc.psum_pool(name="turned", bufs=1) as turned,
     ):
         offsets = held.tile([P, picked // 16], U16, name="offsets")
         nc.sync.dma_start(offsets[:], offs)
-        mask_row = held.tile([1, samples], F32, name="mask_row")
-        nc.scalar.dma_start(mask_row[:], row_mask.rearrange("b one -> one b"))
 
-        p_tiles, c_tiles, y_tiles = [], [], []
+        p_tiles = [loads.tile([P, picked], F32, name="p") for i in range(blocks)]
+        c_tiles = [loads.tile([P, picked], F32, name="c") for i in range(blocks)]
+        y_tiles = [loads.tile([P, classes], F32, name="y") for i in range(blocks)]
         for i in range(blocks):
             rows = slice(i * P, (i + 1) * P)
-            c = loads.tile([P, picked], F32, name="c")
-            p = loads.tile([P, picked], F32, name="p")
-            y = loads.tile([P, classes], F32, name="y")
-            nc.sync.dma_start(c[:], prob_cons[rows, :])
-            nc.sync.dma_start(p[:], prob[rows, :])
-            nc.sync.dma_start(y[:], label[rows, :])
-            c_tiles.append(c)
-            p_tiles.append(p)
-            y_tiles.append(y)
-
-        identity = held.tile([P, P], F32, name="identity")
-        make_identity(nc, identity[:])
-        one = held.tile([1, 1], F32, name="one")
-        nc.vector.memset(one[:], 1.0)
-
-        mask_psum = turned.tile([P, blocks], F32, name="mask_psum")
-        for i in range(blocks):
-            nc.tensor.matmul(mask_psum[:, i : i + 1], mask_row[:, i * P : (i + 1) * P], one[:], start=True, stop=True)
+            nc.sync.dma_start(p_tiles[i][:], prob[rows, :])
+            nc.sync.dma_start(c_tiles[i][:], prob_cons[rows, :])
+            nc.sync.dma_start(y_tiles[i][:], label[rows, :])
         mask = held.tile([P, blocks], F32, name="mask")
-        nc.vector.tensor_copy(mask[:], mask_psum[:])
+        with nc.allow_non_contiguous_dma(reason="one mask value to a partition, 512 in all"):
+            nc.scalar.dma_start(mask[:], row_mask.rearrange("(n p) one -> p (n one)", p=P))
 
-        plus_mask = held.tile([P, blocks, P], F32, name="plus_mask")
-        minus_mask = held.tile([P, blocks, P], F32, name="minus_mask")
-        plus_mask_bf = held.tile([P, blocks, P], BF16, name="plus_mask_bf")
+        plus = held.tile([P, P], F32, name="plus")
+        make_identity(nc, plus[:])
+        minus = held.tile([P, P], F32, name="minus")
+        nc.gpsimd.tensor_scalar(minus[:], plus[:], -1.0, None, ALU.mult)
+        plus_bf = held.tile([P, P], BF16, name="plus_bf")
+        nc.gpsimd.tensor_copy(plus_bf[:], plus[:])
 
-        def finish(i, picked_d, rest):
-            loss = work.tile([P, picked], F32, name="loss")
-            nc.vector.scalar_tensor_tensor(loss[:], picked_d[:], mask[:, i : i + 1], rest[:], ALU.mult, ALU.add)
-            nc.sync.dma_start(out[i * P : (i + 1) * P, :], loss[:])
+        cons_err, picked_d, rest = [], [], []
 
-        waiting = None
-        for i in range(blocks):
-            p, c, y = p_tiles[i], c_tiles[i], y_tiles[i]
-
-            c4 = work.tile([P, picked], F32, name="c4")
-            nc.scalar.mul(c4[:], c[:], 4.0)
-            smooth = work.tile([P, picked], F32, name="smooth")
-            nc.vector.scalar_tensor_tensor(smooth[:], p[:], -3.0, c4[:], ALU.mult, ALU.add)
-            cons_err = work.tile([P, picked], F32, name="cons_err")
-            nc.vector.scalar_tensor_tensor(cons_err[:], p[:], 0.5, smooth[:], ALU.is_gt, ALU.subtract)
-
-            if i == 0:
-                for k in range(blocks):
-                    nc.vector.tensor_scalar(plus_mask[:, k, :], identity[:], mask[:, k : k + 1], None, ALU.mult)
-                nc.vector.tensor_scalar(minus_mask[:], plus_mask[:], -1.0, None, ALU.mult)
-                nc.vector.tensor_copy(plus_mask_bf[:], plus_mask[:])
-            else:
-                finish(*waiting)
-
-            log_p = work.tile([P, picked], F32, name="log_p")
+        def front(i):
+            p = p_tiles[i]
             log_q = work.tile([P, picked], F32, name="log_q")
-            nc.scalar.activation(log_p[:], p[:], ACT.Ln)
             nc.scalar.activation(log_q[:], p[:], ACT.Ln, bias=1.0, scale=-1.0)
+            log_p = work.tile([P, picked], F32, name="log_p")
+            nc.scalar.activation(log_p[:], p[:], ACT.Ln)
+            c4 = work.tile([P, picked], F32, name="c4")
+            nc.scalar.mul(c4[:], c_tiles[i][:], 4.0)
 
             neg_d = work.tile([P, picked], F32, name="neg_d")
             nc.vector.tensor_tensor(neg_d[:], log_q[:], log_p[:], ALU.subtract)
-            picked_d = work.tile([P, picked], F32, name="picked_d")
-            nc.vector.tensor_tensor(picked_d[:], y[:].indirect(offsets[:]), neg_d[:], ALU.mult)
+            smooth = work.tile([P, picked], F32, name="smooth")
+            nc.vector.scalar_tensor_tensor(smooth[:], p[:], -3.0, c4[:], ALU.mult, ALU.add)
+            cons_err.append(work.tile([P, picked], F32, name="cons_err"))
+            nc.vector.scalar_tensor_tensor(cons_err[i][:], p[:], 0.5, smooth[:], ALU.is_gt, ALU.subtract)
+            picked_d.append(work.tile([P, picked], F32, name="picked_d"))
+            nc.vector.tensor_tensor(picked_d[i][:], y_tiles[i][:].indirect(offsets[:]), neg_d[:], ALU.mult)
 
+            rest.append(sums.tile([P, picked], F32, name="rest"))
+            nc.tensor.matmul(rest[i][:], minus[:], log_q[:], start=True, stop=False)
+
+        def back(i):
             sq_cons = work.tile([P, picked], F32, name="sq_cons")
-            nc.scalar.activation(sq_cons[:], cons_err[:], ACT.Square, scale=0.25)
+            nc.scalar.activation(sq_cons[:], cons_err[i][:], ACT.Square, scale=0.25)
             dist = work.tile([P, picked], F32, name="dist")
-            nc.scalar.activation(dist[:], p[:], ACT.Abs, bias=-0.5)
+            nc.scalar.activation(dist[:], p_tiles[i][:], ACT.Abs, bias=-0.5)
             sq_own = work.tile([P, picked], BF16, name="sq_own")
             nc.scalar.activation(sq_own[:], dist[:], ACT.Square, bias=0.125, scale=-0.25)
+            nc.tensor.matmul(rest[i][:], plus[:], sq_cons[:], start=False, stop=False)
+            nc.tensor.matmul(rest[i][:], plus_bf[:], sq_own[:], start=False, stop=True)
 
-            rest = sums.tile([P, picked], F32, name="rest")
-            nc.tensor.matmul(rest[:], minus_mask[:, i, :], log_q[:], start=True, stop=False)
-            nc.tensor.matmul(rest[:], plus_mask[:, i, :], sq_cons[:], start=False, stop=False)
-            nc.tensor.matmul(rest[:], plus_mask_bf[:, i, :], sq_own[:], start=False, stop=True)
-            waiting = (i, picked_d, rest)
-        finish(*waiting)
+        for i in range(blocks + 1):
+            if i < blocks:
+                front(i)
+            if i > 0:
+                back(i - 1)
+        for i in range(blocks):
+            loss = work.tile([P, picked], F32, name="loss")
+            nc.vector.tensor_tensor(loss[:], picked_d[i][:], rest[i][:], ALU.add)
+            nc.vector.tensor_scalar(loss[:], loss[:], mask[:, i : i + 1], None, ALU.mult)
+            nc.sync.dma_start(out[i * P : (i + 1) * P, :], loss[:])

@@ -24,14 +24,15 @@ def tile_semiloss_kernel(tc, label, prob, prob_cons, row_mask, offs, out):
         offsets = held.tile([P, picked // 16], U16, name="offsets")
         nc.sync.dma_start(offsets[:], offs)
 
-        p_tiles = [loads.tile([P, picked], F32, name="p") for i in range(blocks)]
         c_tiles = [loads.tile([P, picked], F32, name="c") for i in range(blocks)]
+        p_tiles = [loads.tile([P, picked], F32, name="p") for i in range(blocks)]
         y_tiles = [loads.tile([P, classes], F32, name="y") for i in range(blocks)]
-        for i in range(blocks):
-            rows = slice(i * P, (i + 1) * P)
-            nc.sync.dma_start(p_tiles[i][:], prob[rows, :])
-            nc.sync.dma_start(c_tiles[i][:], prob_cons[rows, :])
-            nc.sync.dma_start(y_tiles[i][:], label[rows, :])
+        for i in range(blocks + 1):
+            if i < blocks:
+                nc.sync.dma_start(c_tiles[i][:], prob_cons[i * P : (i + 1) * P, :])
+                nc.sync.dma_start(p_tiles[i][:], prob[i * P : (i + 1) * P, :])
+            if i > 0:
+                nc.sync.dma_start(y_tiles[i - 1][:], label[(i - 1) * P : i * P, :])
         mask = held.tile([P, blocks], F32, name="mask")
         with nc.allow_non_contiguous_dma(reason="one mask value to a partition, 512 in all"):
             nc.scalar.dma_start(mask[:], row_mask.rearrange("(n p) one -> p (n one)", p=P))
@@ -43,46 +44,53 @@ def tile_semiloss_kernel(tc, label, prob, prob_cons, row_mask, offs, out):
         plus_bf = held.tile([P, P], BF16, name="plus_bf")
         nc.gpsimd.tensor_copy(plus_bf[:], plus[:])
 
+        one = held.tile([P, 1], F32, name="one")
+        nc.vector.memset(one[:], 1.0)
+        zero = held.tile([P, 1], F32, name="zero")
+        nc.scalar.activation(zero[:], one[:], ACT.Ln)
+
         cons_err, picked_d, rest = [], [], []
 
-        def front(i):
-            p = p_tiles[i]
-            log_q = work.tile([P, picked], F32, name="log_q")
-            nc.scalar.activation(log_q[:], p[:], ACT.Ln, bias=1.0, scale=-1.0)
-            log_p = work.tile([P, picked], F32, name="log_p")
-            nc.scalar.activation(log_p[:], p[:], ACT.Ln)
+        def consistency(i):
             c4 = work.tile([P, picked], F32, name="c4")
             nc.scalar.mul(c4[:], c_tiles[i][:], 4.0)
+            smooth = work.tile([P, picked], F32, name="smooth")
+            nc.vector.scalar_tensor_tensor(smooth[:], p_tiles[i][:], -3.0, c4[:], ALU.mult, ALU.add)
+            cons_err.append(work.tile([P, picked], F32, name="cons_err"))
+            nc.vector.scalar_tensor_tensor(cons_err[i][:], p_tiles[i][:], 0.5, smooth[:], ALU.is_gt, ALU.subtract)
 
+        def entropy(i):
+            log_q = work.tile([P, picked], F32, name="log_q")
+            nc.scalar.activation(log_q[:], p_tiles[i][:], ACT.Ln, bias=1.0, scale=-1.0)
+            log_p = work.tile([P, picked], F32, name="log_p")
+            nc.scalar.activation(log_p[:], p_tiles[i][:], ACT.Ln)
             neg_d = work.tile([P, picked], F32, name="neg_d")
             nc.vector.tensor_tensor(neg_d[:], log_q[:], log_p[:], ALU.subtract)
-            smooth = work.tile([P, picked], F32, name="smooth")
-            nc.vector.scalar_tensor_tensor(smooth[:], p[:], -3.0, c4[:], ALU.mult, ALU.add)
-            cons_err.append(work.tile([P, picked], F32, name="cons_err"))
-            nc.vector.scalar_tensor_tensor(cons_err[i][:], p[:], 0.5, smooth[:], ALU.is_gt, ALU.subtract)
             picked_d.append(work.tile([P, picked], F32, name="picked_d"))
             nc.vector.tensor_tensor(picked_d[i][:], y_tiles[i][:].indirect(offsets[:]), neg_d[:], ALU.mult)
-
             rest.append(sums.tile([P, picked], F32, name="rest"))
             nc.tensor.matmul(rest[i][:], minus[:], log_q[:], start=True, stop=False)
 
-        def back(i):
+        def squares(i):
             sq_cons = work.tile([P, picked], F32, name="sq_cons")
             nc.scalar.activation(sq_cons[:], cons_err[i][:], ACT.Square, scale=0.25)
             dist = work.tile([P, picked], F32, name="dist")
             nc.scalar.activation(dist[:], p_tiles[i][:], ACT.Abs, bias=-0.5)
             sq_own = work.tile([P, picked], BF16, name="sq_own")
             nc.scalar.activation(sq_own[:], dist[:], ACT.Square, bias=0.125, scale=-0.25)
+            nc.vector.tensor_scalar(picked_d[i][:], picked_d[i][:], mask[:, i : i + 1], None, ALU.mult)
             nc.tensor.matmul(rest[i][:], plus[:], sq_cons[:], start=False, stop=False)
             nc.tensor.matmul(rest[i][:], plus_bf[:], sq_own[:], start=False, stop=True)
 
+        consistency(0)
         for i in range(blocks + 1):
+            if i + 1 < blocks:
+                consistency(i + 1)
             if i < blocks:
-                front(i)
+                entropy(i)
             if i > 0:
-                back(i - 1)
+                squares(i - 1)
         for i in range(blocks):
             loss = work.tile([P, picked], F32, name="loss")
-            nc.vector.tensor_tensor(loss[:], picked_d[i][:], rest[i][:], ALU.add)
-            nc.vector.tensor_scalar(loss[:], loss[:], mask[:, i : i + 1], None, ALU.mult)
+            nc.vector.scalar_tensor_tensor(loss[:], rest[i][:], mask[:, i : i + 1], picked_d[i][:], ALU.mult, ALU.add)
             nc.sync.dma_start(out[i * P : (i + 1) * P, :], loss[:])

@@ -37,6 +37,15 @@ def tile_semiloss_kernel(tc, label, prob, prob_cons, row_mask, offs, out):
         with nc.allow_non_contiguous_dma(reason="one mask value to a partition, 512 in all"):
             nc.scalar.dma_start(mask[:], row_mask.rearrange("(n p) one -> p (n one)", p=P))
 
+        neg_mask = held.tile([P, blocks], F32, name="neg_mask")
+        nc.vector.tensor_scalar(neg_mask[:], mask[:], -1.0, None, ALU.mult)
+        unmask = held.tile([P, blocks], F32, name="unmask")
+        nc.vector.tensor_scalar(unmask[:], mask[:], -1.0, 1.0, ALU.mult, ALU.add)
+        quarter = held.tile([P, blocks], F32, name="quarter")
+        nc.vector.tensor_scalar(quarter[:], mask[:], 0.25, None, ALU.mult)
+        neg_eighth = held.tile([P, blocks], F32, name="neg_eighth")
+        nc.vector.tensor_scalar(neg_eighth[:], mask[:], -0.125, None, ALU.mult)
+
         plus = held.tile([P, P], F32, name="plus")
         make_identity(nc, plus[:])
         minus = held.tile([P, P], F32, name="minus")
@@ -60,10 +69,11 @@ def tile_semiloss_kernel(tc, label, prob, prob_cons, row_mask, offs, out):
             nc.vector.scalar_tensor_tensor(cons_err[i][:], p_tiles[i][:], 0.5, smooth[:], ALU.is_gt, ALU.subtract)
 
         def entropy(i):
+            col = slice(i, i + 1)
             log_q = work.tile([P, picked], F32, name="log_q")
-            nc.scalar.activation(log_q[:], p_tiles[i][:], ACT.Ln, bias=1.0, scale=-1.0)
+            nc.scalar.activation(log_q[:], p_tiles[i][:], ACT.Ln, bias=1.0, scale=neg_mask[:, col])
             log_p = work.tile([P, picked], F32, name="log_p")
-            nc.scalar.activation(log_p[:], p_tiles[i][:], ACT.Ln)
+            nc.scalar.activation(log_p[:], p_tiles[i][:], ACT.Ln, bias=unmask[:, col], scale=mask[:, col])
             neg_d = work.tile([P, picked], F32, name="neg_d")
             nc.vector.tensor_tensor(neg_d[:], log_q[:], log_p[:], ALU.subtract)
             picked_d.append(work.tile([P, picked], F32, name="picked_d"))
@@ -72,13 +82,13 @@ def tile_semiloss_kernel(tc, label, prob, prob_cons, row_mask, offs, out):
             nc.tensor.matmul(rest[i][:], minus[:], log_q[:], start=True, stop=False)
 
         def squares(i):
+            col = slice(i, i + 1)
             sq_cons = work.tile([P, picked], F32, name="sq_cons")
-            nc.scalar.activation(sq_cons[:], cons_err[i][:], ACT.Square, scale=0.25)
+            nc.scalar.activation(sq_cons[:], cons_err[i][:], ACT.Square, scale=quarter[:, col])
             dist = work.tile([P, picked], F32, name="dist")
             nc.scalar.activation(dist[:], p_tiles[i][:], ACT.Abs, bias=-0.5)
             sq_own = work.tile([P, picked], BF16, name="sq_own")
-            nc.scalar.activation(sq_own[:], dist[:], ACT.Square, bias=0.125, scale=-0.25)
-            nc.vector.tensor_scalar(picked_d[i][:], picked_d[i][:], mask[:, i : i + 1], None, ALU.mult)
+            nc.scalar.activation(sq_own[:], dist[:], ACT.Square, bias=neg_eighth[:, col], scale=quarter[:, col])
             nc.tensor.matmul(rest[i][:], plus[:], sq_cons[:], start=False, stop=False)
             nc.tensor.matmul(rest[i][:], plus_bf[:], sq_own[:], start=False, stop=True)
 
@@ -92,5 +102,5 @@ def tile_semiloss_kernel(tc, label, prob, prob_cons, row_mask, offs, out):
                 squares(i - 1)
         for i in range(blocks):
             loss = work.tile([P, picked], F32, name="loss")
-            nc.vector.scalar_tensor_tensor(loss[:], rest[i][:], mask[:, i : i + 1], picked_d[i][:], ALU.mult, ALU.add)
+            nc.vector.tensor_tensor(loss[:], rest[i][:], picked_d[i][:], ALU.add)
             nc.sync.dma_start(out[i * P : (i + 1) * P, :], loss[:])

@@ -22,20 +22,23 @@ def tile_semiloss_kernel(tc, label, prob, prob_cons, row_mask, offs, out):
         tc.psum_pool(name="sums", bufs=blocks) as sums,
     ):
         offsets = held.tile([P, picked // 16], U16, name="offsets")
-        nc.sync.dma_start(offsets[:], offs)
-
         c_tiles = [loads.tile([P, picked], F32, name="c") for i in range(blocks)]
         p_tiles = [loads.tile([P, picked], F32, name="p") for i in range(blocks)]
         y_tiles = [loads.tile([P, classes], F32, name="y") for i in range(blocks)]
+        prob_blocks = prob.rearrange("(p n) j -> p n j", n=blocks)
+        cons_blocks = prob_cons.rearrange("(p n) j -> p n j", n=blocks)
+        label_blocks = label.rearrange("(p n) s -> p n s", n=blocks)
+        out_blocks = out.rearrange("(p n) j -> p n j", n=blocks)
         for i in range(blocks + 1):
             if i < blocks:
-                nc.sync.dma_start(c_tiles[i][:], prob_cons[i * P : (i + 1) * P, :])
-                nc.sync.dma_start(p_tiles[i][:], prob[i * P : (i + 1) * P, :])
+                nc.sync.dma_start(p_tiles[i][:], prob_blocks[:, i, :])
+                nc.sync.dma_start(c_tiles[i][:], cons_blocks[:, i, :])
+            if i == 0:
+                nc.sync.dma_start(offsets[:], offs)
             if i > 0:
-                nc.sync.dma_start(y_tiles[i - 1][:], label[(i - 1) * P : i * P, :])
+                nc.sync.dma_start(y_tiles[i - 1][:], label_blocks[:, i - 1, :])
         mask = held.tile([P, blocks], F32, name="mask")
-        with nc.allow_non_contiguous_dma(reason="one mask value to a partition, 512 in all"):
-            nc.scalar.dma_start(mask[:], row_mask.rearrange("(n p) one -> p (n one)", p=P))
+        nc.scalar.dma_start(mask[:], row_mask.rearrange("(p n) one -> p (n one)", n=blocks))
 
         neg_mask = held.tile([P, blocks], F32, name="neg_mask")
         nc.vector.tensor_scalar(neg_mask[:], mask[:], -1.0, None, ALU.mult)
@@ -59,6 +62,14 @@ def tile_semiloss_kernel(tc, label, prob, prob_cons, row_mask, offs, out):
         nc.scalar.activation(zero[:], one[:], ACT.Ln)
 
         cons_err, picked_d, rest = [], [], []
+
+        def first_consistency():
+            step = work.tile([P, picked], F32, name="step")
+            nc.vector.tensor_scalar(step[:], p_tiles[0][:], 0.5, None, ALU.is_gt)
+            smooth = work.tile([P, picked], F32, name="smooth")
+            nc.vector.scalar_tensor_tensor(smooth[:], p_tiles[0][:], -0.75, c_tiles[0][:], ALU.mult, ALU.add)
+            cons_err.append(work.tile([P, picked], F32, name="cons_err"))
+            nc.vector.scalar_tensor_tensor(cons_err[0][:], smooth[:], 4.0, step[:], ALU.mult, ALU.subtract)
 
         def consistency(i):
             c4 = work.tile([P, picked], F32, name="c4")
@@ -92,7 +103,7 @@ def tile_semiloss_kernel(tc, label, prob, prob_cons, row_mask, offs, out):
             nc.tensor.matmul(rest[i][:], plus[:], sq_cons[:], start=False, stop=False)
             nc.tensor.matmul(rest[i][:], plus_bf[:], sq_own[:], start=False, stop=True)
 
-        consistency(0)
+        first_consistency()
         for i in range(blocks + 1):
             if i + 1 < blocks:
                 consistency(i + 1)
@@ -103,4 +114,4 @@ def tile_semiloss_kernel(tc, label, prob, prob_cons, row_mask, offs, out):
         for i in range(blocks):
             loss = work.tile([P, picked], F32, name="loss")
             nc.vector.tensor_tensor(loss[:], rest[i][:], picked_d[i][:], ALU.add)
-            nc.sync.dma_start(out[i * P : (i + 1) * P, :], loss[:])
+            nc.sync.dma_start(out_blocks[:, i, :], loss[:])

@@ -63,6 +63,9 @@ def tile_semiloss_kernel(tc, label, prob, prob_cons, row_mask, offs, out):
 
         cons_err, picked_d, rest = [], [], []
 
+        def summed_by_tensor(i):
+            return i < blocks // 2
+
         def first_consistency():
             step = work.tile([P, picked], F32, name="step")
             nc.vector.tensor_scalar(step[:], p_tiles[0][:], 0.5, None, ALU.is_gt)
@@ -94,14 +97,23 @@ def tile_semiloss_kernel(tc, label, prob, prob_cons, row_mask, offs, out):
 
         def squares(i):
             col = slice(i, i + 1)
-            sq_cons = work.tile([P, picked], F32, name="sq_cons")
+            sq_cons = work.tile([P, picked], BF16, name="sq_cons")
             nc.scalar.activation(sq_cons[:], cons_err[i][:], ACT.Square, scale=quarter[:, col])
             dist = work.tile([P, picked], F32, name="dist")
             nc.scalar.activation(dist[:], p_tiles[i][:], ACT.Abs, bias=-0.5)
             sq_own = work.tile([P, picked], BF16, name="sq_own")
             nc.scalar.activation(sq_own[:], dist[:], ACT.Square, bias=neg_eighth[:, col], scale=quarter[:, col])
-            nc.tensor.matmul(rest[i][:], plus[:], sq_cons[:], start=False, stop=False)
-            nc.tensor.matmul(rest[i][:], plus_bf[:], sq_own[:], start=False, stop=True)
+            nc.tensor.matmul(rest[i][:], plus_bf[:], sq_cons[:], start=False, stop=False)
+            nc.tensor.matmul(rest[i][:], plus_bf[:], sq_own[:], start=False, stop=not summed_by_tensor(i))
+
+        def finish(i):
+            loss = work.tile([P, picked], F32, name="loss")
+            if summed_by_tensor(i):
+                nc.tensor.matmul(rest[i][:], plus[:], picked_d[i][:], start=False, stop=True)
+                nc.scalar.copy(loss[:], rest[i][:])
+            else:
+                nc.vector.tensor_tensor(loss[:], rest[i][:], picked_d[i][:], ALU.add)
+            nc.sync.dma_start(out_blocks[:, i, :], loss[:])
 
         first_consistency()
         for i in range(blocks + 1):
@@ -111,7 +123,8 @@ def tile_semiloss_kernel(tc, label, prob, prob_cons, row_mask, offs, out):
                 entropy(i)
             if i > 0:
                 squares(i - 1)
+                if summed_by_tensor(i - 1):
+                    finish(i - 1)
         for i in range(blocks):
-            loss = work.tile([P, picked], F32, name="loss")
-            nc.vector.tensor_tensor(loss[:], rest[i][:], picked_d[i][:], ALU.add)
-            nc.sync.dma_start(out_blocks[:, i, :], loss[:])
+            if not summed_by_tensor(i):
+                finish(i)

@@ -1,11 +1,13 @@
+import math
+
 import concourse.mybir as mybir
-from concourse.masks import make_identity
 
 F32 = mybir.dt.float32
 U16 = mybir.dt.uint16
 ALU = mybir.AluOpType
 ACT = mybir.ActivationFunctionType
 P = 128
+SQUARE = 32
 BF16 = mybir.dt.bfloat16
 
 
@@ -20,7 +22,11 @@ def tile_semiloss_kernel(tc, label, prob, prob_cons, row_mask, offs, out):
         tc.tile_pool(name="loads", bufs=blocks) as loads,
         tc.tile_pool(name="work", bufs=blocks) as work,
         tc.psum_pool(name="sums", bufs=blocks) as sums,
+        tc.psum_pool(name="brief", bufs=2) as brief,
     ):
+        mask = held.tile([P, blocks], F32, name="mask")
+        nc.scalar.dma_start(mask[:], row_mask.rearrange("(p n) one -> p (n one)", n=blocks))
+
         offsets = held.tile([P, picked // 16], U16, name="offsets")
         c_tiles = [loads.tile([P, picked], F32, name="c") for i in range(blocks)]
         p_tiles = [loads.tile([P, picked], F32, name="p") for i in range(blocks)]
@@ -29,102 +35,97 @@ def tile_semiloss_kernel(tc, label, prob, prob_cons, row_mask, offs, out):
         cons_blocks = prob_cons.rearrange("(p n) j -> p n j", n=blocks)
         label_blocks = label.rearrange("(p n) s -> p n s", n=blocks)
         out_blocks = out.rearrange("(p n) j -> p n j", n=blocks)
-        for i in range(blocks + 1):
-            if i < blocks:
-                nc.sync.dma_start(p_tiles[i][:], prob_blocks[:, i, :])
-                nc.sync.dma_start(c_tiles[i][:], cons_blocks[:, i, :])
-            if i == 0:
-                nc.sync.dma_start(offsets[:], offs)
-            if i > 0:
-                nc.sync.dma_start(y_tiles[i - 1][:], label_blocks[:, i - 1, :])
-        mask = held.tile([P, blocks], F32, name="mask")
-        nc.scalar.dma_start(mask[:], row_mask.rearrange("(p n) one -> p (n one)", n=blocks))
+        for i in range(blocks):
+            nc.sync.dma_start(p_tiles[i][:], prob_blocks[:, i, :])
+            nc.sync.dma_start(c_tiles[i][:], cons_blocks[:, i, :])
+        nc.sync.dma_start(offsets[:], offs)
+        for i in range(blocks):
+            nc.sync.dma_start(y_tiles[i][:], label_blocks[:, i, :])
+        ones = held.tile([P, SQUARE], F32, name="ones")
+        nc.vector.memset(ones[:], 1.0)
+        column = held.tile([P, SQUARE], F32, name="column", align_bytes=64)
+        nc.vector.tensor_tensor_scan(column[:], ones[:], ones[:], 0.0, ALU.mult, ALU.add)
+        row = held.tile([P, SQUARE], F32, name="row", align_bytes=64)
+        nc.vector.transpose(row[:], column[:])
+        plus = held.tile([P, P], BF16, name="plus")
+        nc.vector.memset(plus[:], 0.0)
+        for start in range(0, P, SQUARE):
+            part = slice(start, start + SQUARE)
+            nc.vector.tensor_tensor(plus[part, part], column[part, :], row[part, :], ALU.is_equal)
+        minus = held.tile([P, P], BF16, name="minus")
+        nc.vector.tensor_scalar(minus[:], plus[:], -1.0, None, ALU.mult)
+        neg_quarter = held.tile([P, P], BF16, name="neg_quarter")
+        nc.vector.tensor_scalar(neg_quarter[:], plus[:], -0.25, None, ALU.mult)
 
-        neg_mask = held.tile([P, blocks], F32, name="neg_mask")
-        nc.vector.tensor_scalar(neg_mask[:], mask[:], -1.0, None, ALU.mult)
+        twice = held.tile([P, blocks], F32, name="twice")
+        nc.vector.tensor_scalar(twice[:], mask[:], 2.0, None, ALU.mult)
+        neg_twice = held.tile([P, blocks], F32, name="neg_twice")
+        nc.vector.tensor_scalar(neg_twice[:], mask[:], -2.0, None, ALU.mult)
+        one_more = held.tile([P, blocks], F32, name="one_more")
+        nc.vector.tensor_scalar(one_more[:], mask[:], 1.0, None, ALU.add)
         unmask = held.tile([P, blocks], F32, name="unmask")
         nc.vector.tensor_scalar(unmask[:], mask[:], -1.0, 1.0, ALU.mult, ALU.add)
         quarter = held.tile([P, blocks], F32, name="quarter")
         nc.vector.tensor_scalar(quarter[:], mask[:], 0.25, None, ALU.mult)
-        neg_eighth = held.tile([P, blocks], F32, name="neg_eighth")
-        nc.vector.tensor_scalar(neg_eighth[:], mask[:], -0.125, None, ALU.mult)
+        log_2 = held.tile([P, blocks], F32, name="log_2")
+        nc.vector.tensor_scalar(log_2[:], mask[:], math.log(2.0), None, ALU.mult)
 
-        plus = held.tile([P, P], F32, name="plus")
-        make_identity(nc, plus[:])
-        minus = held.tile([P, P], F32, name="minus")
-        nc.gpsimd.tensor_scalar(minus[:], plus[:], -1.0, None, ALU.mult)
-        plus_bf = held.tile([P, P], BF16, name="plus_bf")
-        nc.gpsimd.tensor_copy(plus_bf[:], plus[:])
-
-        one = held.tile([P, 1], F32, name="one")
-        nc.vector.memset(one[:], 1.0)
         zero = held.tile([P, 1], F32, name="zero")
-        nc.scalar.activation(zero[:], one[:], ACT.Ln)
+        nc.scalar.activation(zero[:], ones[:, 0:1], ACT.Ln)
 
-        cons_err, picked_d, rest = [], [], []
-
-        def summed_by_tensor(i):
-            return i < blocks // 2
-
-        def first_consistency():
-            step = work.tile([P, picked], F32, name="step")
-            nc.vector.tensor_scalar(step[:], p_tiles[0][:], 0.5, None, ALU.is_gt)
-            smooth = work.tile([P, picked], F32, name="smooth")
-            nc.vector.scalar_tensor_tensor(smooth[:], p_tiles[0][:], -0.75, c_tiles[0][:], ALU.mult, ALU.add)
-            cons_err.append(work.tile([P, picked], F32, name="cons_err"))
-            nc.vector.scalar_tensor_tensor(cons_err[0][:], smooth[:], 4.0, step[:], ALU.mult, ALU.subtract)
+        neg_edge, shift, log_ratio, rest, cons_err, neg_d, picked_d = [], [], [], [], [], [], []
 
         def consistency(i):
-            c4 = work.tile([P, picked], F32, name="c4")
-            nc.scalar.mul(c4[:], c_tiles[i][:], 4.0)
-            smooth = work.tile([P, picked], F32, name="smooth")
-            nc.vector.scalar_tensor_tensor(smooth[:], p_tiles[i][:], -3.0, c4[:], ALU.mult, ALU.add)
-            cons_err.append(work.tile([P, picked], F32, name="cons_err"))
-            nc.vector.scalar_tensor_tensor(cons_err[i][:], p_tiles[i][:], 0.5, smooth[:], ALU.is_gt, ALU.subtract)
+            neg_edge.append(work.tile([P, picked], BF16, name="neg_edge"))
+            nc.vector.scalar_tensor_tensor(neg_edge[i][:], p_tiles[i][:], 0.5, p_tiles[i][:], ALU.is_gt, ALU.subtract)
+            shift.append(work.tile([P, picked], BF16, name="shift"))
+            nc.vector.tensor_tensor(shift[i][:], c_tiles[i][:], p_tiles[i][:], ALU.subtract)
 
         def entropy(i):
             col = slice(i, i + 1)
-            log_q = work.tile([P, picked], F32, name="log_q")
-            nc.scalar.activation(log_q[:], p_tiles[i][:], ACT.Ln, bias=1.0, scale=neg_mask[:, col])
-            log_p = work.tile([P, picked], F32, name="log_p")
-            nc.scalar.activation(log_p[:], p_tiles[i][:], ACT.Ln, bias=unmask[:, col], scale=mask[:, col])
-            neg_d = work.tile([P, picked], F32, name="neg_d")
-            nc.vector.tensor_tensor(neg_d[:], log_q[:], log_p[:], ALU.subtract)
-            picked_d.append(work.tile([P, picked], F32, name="picked_d"))
-            nc.vector.tensor_tensor(picked_d[i][:], y_tiles[i][:].indirect(offsets[:]), neg_d[:], ALU.mult)
+            log_q = work.tile([P, picked], BF16, name="log_q")
+            nc.scalar.activation(log_q[:], p_tiles[i][:], ACT.Ln, bias=one_more[:, col], scale=neg_twice[:, col])
+            log_p = work.tile([P, picked], BF16, name="log_p")
+            nc.scalar.activation(log_p[:], p_tiles[i][:], ACT.Ln, bias=unmask[:, col], scale=twice[:, col])
+            log_ratio.append(brief.tile([P, picked], F32, name="log_ratio"))
+            nc.tensor.matmul(log_ratio[i][:], plus[:], log_q[:], start=True, stop=False)
+            nc.tensor.matmul(log_ratio[i][:], minus[:], log_p[:], start=False, stop=True)
             rest.append(sums.tile([P, picked], F32, name="rest"))
             nc.tensor.matmul(rest[i][:], minus[:], log_q[:], start=True, stop=False)
-
-        def squares(i):
-            col = slice(i, i + 1)
-            sq_cons = work.tile([P, picked], BF16, name="sq_cons")
-            nc.scalar.activation(sq_cons[:], cons_err[i][:], ACT.Square, scale=quarter[:, col])
-            dist = work.tile([P, picked], F32, name="dist")
-            nc.scalar.activation(dist[:], p_tiles[i][:], ACT.Abs, bias=-0.5)
             sq_own = work.tile([P, picked], BF16, name="sq_own")
-            nc.scalar.activation(sq_own[:], dist[:], ACT.Square, bias=neg_eighth[:, col], scale=quarter[:, col])
-            nc.tensor.matmul(rest[i][:], plus_bf[:], sq_cons[:], start=False, stop=False)
-            nc.tensor.matmul(rest[i][:], plus_bf[:], sq_own[:], start=False, stop=not summed_by_tensor(i))
+            nc.scalar.activation(sq_own[:], neg_edge[i][:], ACT.Square, scale=quarter[:, col])
+            nc.tensor.matmul(rest[i][:], plus[:], sq_own[:], start=False, stop=False)
+
+        def copy_and_distance(i):
+            neg_d.append(work.tile([P, picked], F32, name="neg_d"))
+            nc.scalar.copy(neg_d[i][:], log_ratio[i][:])
+            cons_err.append(brief.tile([P, picked], F32, name="cons_err"))
+            nc.tensor.matmul(cons_err[i][:], neg_quarter[:], neg_edge[i][:], start=True, stop=False)
+            nc.tensor.matmul(cons_err[i][:], plus[:], shift[i][:], start=False, stop=True)
+
+        def last_square(i):
+            sq_cons = work.tile([P, picked], BF16, name="sq_cons")
+            nc.scalar.activation(sq_cons[:], cons_err[i][:], ACT.Square, scale=mask[:, i : i + 1])
+            nc.tensor.matmul(rest[i][:], plus[:], sq_cons[:], start=False, stop=True)
+
+        def gather(i):
+            picked_d.append(work.tile([P, picked], F32, name="picked_d"))
+            nc.vector.tensor_tensor(picked_d[i][:], y_tiles[i][:].indirect(offsets[:]), neg_d[i][:], ALU.mult)
 
         def finish(i):
             loss = work.tile([P, picked], F32, name="loss")
-            if summed_by_tensor(i):
-                nc.tensor.matmul(rest[i][:], plus[:], picked_d[i][:], start=False, stop=True)
-                nc.scalar.copy(loss[:], rest[i][:])
-            else:
-                nc.vector.tensor_tensor(loss[:], rest[i][:], picked_d[i][:], ALU.add)
+            nc.vector.scalar_tensor_tensor(loss[:], rest[i][:], log_2[:, i : i + 1], picked_d[i][:], ALU.add, ALU.add)
             nc.sync.dma_start(out_blocks[:, i, :], loss[:])
 
-        first_consistency()
-        for i in range(blocks + 1):
-            if i + 1 < blocks:
-                consistency(i + 1)
-            if i < blocks:
-                entropy(i)
-            if i > 0:
-                squares(i - 1)
-                if summed_by_tensor(i - 1):
-                    finish(i - 1)
+        for step in range(blocks + 2):
+            if step < blocks:
+                consistency(step)
+                entropy(step)
+            if 0 <= step - 1 < blocks:
+                copy_and_distance(step - 1)
+            if 0 <= step - 2:
+                last_square(step - 2)
         for i in range(blocks):
-            if not summed_by_tensor(i):
-                finish(i)
+            gather(i)
+        for i in range(blocks):
+            finish(i)

@@ -52,6 +52,8 @@ def tile_semiloss_kernel(tc, label, prob, prob_cons, row_mask, offs, out):
         for start in range(0, P, SQUARE):
             part = slice(start, start + SQUARE)
             nc.vector.tensor_tensor(plus[part, part], column[part, :], row[part, :], ALU.is_equal)
+        plus_wide = held.tile([P, P], F32, name="plus_wide")
+        nc.vector.tensor_copy(plus_wide[:], plus[:])
         minus = held.tile([P, P], BF16, name="minus")
         nc.vector.tensor_scalar(minus[:], plus[:], -1.0, None, ALU.mult)
         neg_quarter = held.tile([P, P], BF16, name="neg_quarter")
@@ -73,7 +75,8 @@ def tile_semiloss_kernel(tc, label, prob, prob_cons, row_mask, offs, out):
         zero = held.tile([P, 1], F32, name="zero")
         nc.scalar.activation(zero[:], ones[:, 0:1], ACT.Ln)
 
-        neg_edge, shift, log_ratio, rest, cons_err, neg_d, picked_d = [], [], [], [], [], [], []
+        neg_edge, shift, neg_d, rest, picked_d = [], [], [], [], []
+        log_ratio = {}
 
         def consistency(i):
             neg_edge.append(work.tile([P, picked], BF16, name="neg_edge"))
@@ -84,29 +87,38 @@ def tile_semiloss_kernel(tc, label, prob, prob_cons, row_mask, offs, out):
         def entropy(i):
             col = slice(i, i + 1)
             log_q = work.tile([P, picked], BF16, name="log_q")
-            nc.scalar.activation(log_q[:], p_tiles[i][:], ACT.Ln, bias=one_more[:, col], scale=neg_twice[:, col])
             log_p = work.tile([P, picked], BF16, name="log_p")
-            nc.scalar.activation(log_p[:], p_tiles[i][:], ACT.Ln, bias=unmask[:, col], scale=twice[:, col])
-            log_ratio.append(brief.tile([P, picked], F32, name="log_ratio"))
-            nc.tensor.matmul(log_ratio[i][:], plus[:], log_q[:], start=True, stop=False)
-            nc.tensor.matmul(log_ratio[i][:], minus[:], log_p[:], start=False, stop=True)
+            if i == 0:
+                nc.scalar.activation(log_q[:], p_tiles[i][:], ACT.Ln, bias=2.0, scale=-2.0)
+                nc.scalar.activation(log_p[:], p_tiles[i][:], ACT.Ln, bias=0.0, scale=2.0)
+            else:
+                nc.scalar.activation(log_q[:], p_tiles[i][:], ACT.Ln, bias=one_more[:, col], scale=neg_twice[:, col])
+                nc.scalar.activation(log_p[:], p_tiles[i][:], ACT.Ln, bias=unmask[:, col], scale=twice[:, col])
+            neg_d.append(work.tile([P, picked], F32, name="neg_d"))
+            if i == 0:
+                nc.vector.tensor_tensor(neg_d[i][:], log_q[:], log_p[:], ALU.subtract)
+            else:
+                log_ratio[i] = brief.tile([P, picked], F32, name="log_ratio")
+                nc.tensor.matmul(log_ratio[i][:], plus[:], log_q[:], start=True, stop=False)
+                nc.tensor.matmul(log_ratio[i][:], minus[:], log_p[:], start=False, stop=True)
             rest.append(sums.tile([P, picked], F32, name="rest"))
             nc.tensor.matmul(rest[i][:], minus[:], log_q[:], start=True, stop=False)
+
+        def copy_d(i):
+            if i > 0:
+                nc.scalar.copy(neg_d[i][:], log_ratio[i][:])
+
+        def squares(i):
+            col = slice(i, i + 1)
+            cons_err = brief.tile([P, picked], F32, name="cons_err")
+            nc.tensor.matmul(cons_err[:], neg_quarter[:], neg_edge[i][:], start=True, stop=False)
+            nc.tensor.matmul(cons_err[:], plus[:], shift[i][:], start=False, stop=True)
             sq_own = work.tile([P, picked], BF16, name="sq_own")
-            nc.scalar.activation(sq_own[:], neg_edge[i][:], ACT.Square, scale=quarter[:, col])
+            nc.scalar.activation(sq_own[:], neg_edge[i][:], ACT.Square, scale=0.25 if i == 0 else quarter[:, col])
             nc.tensor.matmul(rest[i][:], plus[:], sq_own[:], start=False, stop=False)
-
-        def copy_and_distance(i):
-            neg_d.append(work.tile([P, picked], F32, name="neg_d"))
-            nc.scalar.copy(neg_d[i][:], log_ratio[i][:])
-            cons_err.append(brief.tile([P, picked], F32, name="cons_err"))
-            nc.tensor.matmul(cons_err[i][:], neg_quarter[:], neg_edge[i][:], start=True, stop=False)
-            nc.tensor.matmul(cons_err[i][:], plus[:], shift[i][:], start=False, stop=True)
-
-        def last_square(i):
             sq_cons = work.tile([P, picked], BF16, name="sq_cons")
-            nc.scalar.activation(sq_cons[:], cons_err[i][:], ACT.Square, scale=mask[:, i : i + 1])
-            nc.tensor.matmul(rest[i][:], plus[:], sq_cons[:], start=False, stop=True)
+            nc.scalar.activation(sq_cons[:], cons_err[:], ACT.Square, scale=1.0 if i == 0 else mask[:, col])
+            nc.tensor.matmul(rest[i][:], plus[:], sq_cons[:], start=False, stop=i > 0)
 
         def gather(i):
             picked_d.append(work.tile([P, picked], F32, name="picked_d"))
@@ -114,17 +126,23 @@ def tile_semiloss_kernel(tc, label, prob, prob_cons, row_mask, offs, out):
 
         def finish(i):
             loss = work.tile([P, picked], F32, name="loss")
-            nc.vector.scalar_tensor_tensor(loss[:], rest[i][:], log_2[:, i : i + 1], picked_d[i][:], ALU.add, ALU.add)
+            if i == 0:
+                col = slice(i, i + 1)
+                nc.tensor.matmul(rest[i][:], plus_wide[:], picked_d[i][:], start=False, stop=True)
+                nc.scalar.activation(loss[:], rest[i][:], ACT.Identity, bias=log_2[:, col], scale=mask[:, col])
+            else:
+                nc.vector.scalar_tensor_tensor(
+                    loss[:], rest[i][:], log_2[:, i : i + 1], picked_d[i][:], ALU.add, ALU.add
+                )
             nc.sync.dma_start(out_blocks[:, i, :], loss[:])
 
-        for step in range(blocks + 2):
+        for step in range(blocks + 1):
             if step < blocks:
                 consistency(step)
                 entropy(step)
-            if 0 <= step - 1 < blocks:
-                copy_and_distance(step - 1)
-            if 0 <= step - 2:
-                last_square(step - 2)
+            if step > 0:
+                copy_d(step - 1)
+                squares(step - 1)
         for i in range(blocks):
             gather(i)
         for i in range(blocks):

@@ -120,21 +120,29 @@ def tile_semiloss_kernel(tc, label, prob, prob_cons, row_mask, offs, out):
             nc.scalar.activation(sq_cons[:], cons_err[:], ACT.Square, scale=1.0 if i == 0 else mask[:, col])
             nc.tensor.matmul(rest[i][:], plus[:], sq_cons[:], start=False, stop=i > 0)
 
+        def parts(i):
+            pieces = 2 if i == blocks - 1 else 1
+            return [slice(k * picked // pieces, (k + 1) * picked // pieces) for k in range(pieces)]
+
         def gather(i):
             picked_d.append(work.tile([P, picked], F32, name="picked_d"))
-            nc.vector.tensor_tensor(picked_d[i][:], y_tiles[i][:].indirect(offsets[:]), neg_d[i][:], ALU.mult)
+            for part in parts(i):
+                looked_up = y_tiles[i][:].indirect(offsets[:, part.start // 16 : part.stop // 16])
+                nc.vector.tensor_tensor(picked_d[i][:, part], looked_up, neg_d[i][:, part], ALU.mult)
 
         def finish(i):
             loss = work.tile([P, picked], F32, name="loss")
+            col = slice(i, i + 1)
             if i == 0:
-                col = slice(i, i + 1)
                 nc.tensor.matmul(rest[i][:], plus_wide[:], picked_d[i][:], start=False, stop=True)
                 nc.scalar.activation(loss[:], rest[i][:], ACT.Identity, bias=log_2[:, col], scale=mask[:, col])
             else:
-                nc.vector.scalar_tensor_tensor(
-                    loss[:], rest[i][:], log_2[:, i : i + 1], picked_d[i][:], ALU.add, ALU.add
-                )
-            nc.sync.dma_start(out_blocks[:, i, :], loss[:])
+                for part in parts(i):
+                    nc.vector.scalar_tensor_tensor(
+                        loss[:, part], rest[i][:, part], log_2[:, col], picked_d[i][:, part], ALU.add, ALU.add
+                    )
+            for part in parts(i):
+                nc.sync.dma_start(out_blocks[:, i, part], loss[:, part])
 
         for step in range(blocks + 1):
             if step < blocks:

@@ -144,13 +144,12 @@ def tile_semiloss_kernel(tc, label, prob, prob_cons, row_mask, offs, out):
             for part in parts(i):
                 nc.sync.dma_start(out_blocks[:, i, part], loss[:, part])
 
-        for step in range(blocks + 1):
-            if step < blocks:
-                consistency(step)
-                entropy(step)
-            if step > 0:
-                copy_d(step - 1)
-                squares(step - 1)
+        for i in range(blocks):
+            consistency(i)
+            entropy(i)
+        for i in range(blocks):
+            copy_d(i)
+            squares(i)
         for i in range(blocks):
             gather(i)
         for i in range(blocks):

@@ -150,7 +150,9 @@ def tile_semiloss_kernel(tc, label, prob, prob_cons, row_mask, offs, out):
         for i in range(blocks):
             copy_d(i)
             squares(i)
-        for i in range(blocks):
+        for i in range(blocks - 1):
             gather(i)
-        for i in range(blocks):
+        for i in range(blocks - 1):
             finish(i)
+        gather(blocks - 1)
+        finish(blocks - 1)

import math

import concourse.mybir as mybir

F32 = mybir.dt.float32
U16 = mybir.dt.uint16
ALU = mybir.AluOpType
ACT = mybir.ActivationFunctionType
P = 128
SQUARE = 32
BF16 = mybir.dt.bfloat16


def tile_semiloss_kernel(tc, label, prob, prob_cons, row_mask, offs, out):
    nc = tc.nc
    samples, classes = label.shape
    picked = prob.shape[1]
    blocks = samples // P

    with (
        tc.tile_pool(name="held", bufs=1) as held,
        tc.tile_pool(name="loads", bufs=blocks) as loads,
        tc.tile_pool(name="work", bufs=blocks) as work,
        tc.psum_pool(name="sums", bufs=blocks) as sums,
        tc.psum_pool(name="brief", bufs=2) as brief,
    ):
        mask = held.tile([P, blocks], F32, name="mask")
        nc.scalar.dma_start(mask[:], row_mask.rearrange("(p n) one -> p (n one)", n=blocks))

        offsets = held.tile([P, picked // 16], U16, name="offsets")
        c_tiles = [loads.tile([P, picked], F32, name="c") for i in range(blocks)]
        p_tiles = [loads.tile([P, picked], F32, name="p") for i in range(blocks)]
        y_tiles = [loads.tile([P, classes], F32, name="y") for i in range(blocks)]
        prob_blocks = prob.rearrange("(p n) j -> p n j", n=blocks)
        cons_blocks = prob_cons.rearrange("(p n) j -> p n j", n=blocks)
        label_blocks = label.rearrange("(p n) s -> p n s", n=blocks)
        out_blocks = out.rearrange("(p n) j -> p n j", n=blocks)
        for i in range(blocks):
            nc.sync.dma_start(p_tiles[i][:], prob_blocks[:, i, :])
            nc.sync.dma_start(c_tiles[i][:], cons_blocks[:, i, :])
        nc.sync.dma_start(offsets[:], offs)
        for i in range(blocks):
            nc.sync.dma_start(y_tiles[i][:], label_blocks[:, i, :])
        ones = held.tile([P, SQUARE], F32, name="ones")
        nc.vector.memset(ones[:], 1.0)
        column = held.tile([P, SQUARE], F32, name="column", align_bytes=64)
        nc.vector.tensor_tensor_scan(column[:], ones[:], ones[:], 0.0, ALU.mult, ALU.add)
        row = held.tile([P, SQUARE], F32, name="row", align_bytes=64)
        nc.vector.transpose(row[:], column[:])
        plus = held.tile([P, P], BF16, name="plus")
        nc.vector.memset(plus[:], 0.0)
        for start in range(0, P, SQUARE):
            part = slice(start, start + SQUARE)
            nc.vector.tensor_tensor(plus[part, part], column[part, :], row[part, :], ALU.is_equal)
        plus_wide = held.tile([P, P], F32, name="plus_wide")
        nc.vector.tensor_copy(plus_wide[:], plus[:])
        minus = held.tile([P, P], BF16, name="minus")
        nc.vector.tensor_scalar(minus[:], plus[:], -1.0, None, ALU.mult)
        neg_quarter = held.tile([P, P], BF16, name="neg_quarter")
        nc.vector.tensor_scalar(neg_quarter[:], plus[:], -0.25, None, ALU.mult)

        twice = held.tile([P, blocks], F32, name="twice")
        nc.vector.tensor_scalar(twice[:], mask[:], 2.0, None, ALU.mult)
        neg_twice = held.tile([P, blocks], F32, name="neg_twice")
        nc.vector.tensor_scalar(neg_twice[:], mask[:], -2.0, None, ALU.mult)
        one_more = held.tile([P, blocks], F32, name="one_more")
        nc.vector.tensor_scalar(one_more[:], mask[:], 1.0, None, ALU.add)
        unmask = held.tile([P, blocks], F32, name="unmask")
        nc.vector.tensor_scalar(unmask[:], mask[:], -1.0, 1.0, ALU.mult, ALU.add)
        quarter = held.tile([P, blocks], F32, name="quarter")
        nc.vector.tensor_scalar(quarter[:], mask[:], 0.25, None, ALU.mult)
        log_2 = held.tile([P, blocks], F32, name="log_2")
        nc.vector.tensor_scalar(log_2[:], mask[:], math.log(2.0), None, ALU.mult)

        zero = held.tile([P, 1], F32, name="zero")
        nc.scalar.activation(zero[:], ones[:, 0:1], ACT.Ln)

        neg_edge, shift, neg_d, rest, picked_d = [], [], [], [], []
        log_ratio = {}

        def consistency(i):
            neg_edge.append(work.tile([P, picked], BF16, name="neg_edge"))
            nc.vector.scalar_tensor_tensor(neg_edge[i][:], p_tiles[i][:], 0.5, p_tiles[i][:], ALU.is_gt, ALU.subtract)
            shift.append(work.tile([P, picked], BF16, name="shift"))
            nc.vector.tensor_tensor(shift[i][:], c_tiles[i][:], p_tiles[i][:], ALU.subtract)

        def entropy(i):
            col = slice(i, i + 1)
            log_q = work.tile([P, picked], BF16, name="log_q")
            log_p = work.tile([P, picked], BF16, name="log_p")
            if i == 0:
                nc.scalar.activation(log_q[:], p_tiles[i][:], ACT.Ln, bias=2.0, scale=-2.0)
                nc.scalar.activation(log_p[:], p_tiles[i][:], ACT.Ln, bias=0.0, scale=2.0)
            else:
                nc.scalar.activation(log_q[:], p_tiles[i][:], ACT.Ln, bias=one_more[:, col], scale=neg_twice[:, col])
                nc.scalar.activation(log_p[:], p_tiles[i][:], ACT.Ln, bias=unmask[:, col], scale=twice[:, col])
            neg_d.append(work.tile([P, picked], F32, name="neg_d"))
            if i == 0:
                nc.vector.tensor_tensor(neg_d[i][:], log_q[:], log_p[:], ALU.subtract)
            else:
                log_ratio[i] = brief.tile([P, picked], F32, name="log_ratio")
                nc.tensor.matmul(log_ratio[i][:], plus[:], log_q[:], start=True, stop=False)
                nc.tensor.matmul(log_ratio[i][:], minus[:], log_p[:], start=False, stop=True)
            rest.append(sums.tile([P, picked], F32, name="rest"))
            nc.tensor.matmul(rest[i][:], minus[:], log_q[:], start=True, stop=False)

        def copy_d(i):
            if i > 0:
                nc.scalar.copy(neg_d[i][:], log_ratio[i][:])

        def squares(i):
            col = slice(i, i + 1)
            cons_err = brief.tile([P, picked], F32, name="cons_err")
            nc.tensor.matmul(cons_err[:], neg_quarter[:], neg_edge[i][:], start=True, stop=False)
            nc.tensor.matmul(cons_err[:], plus[:], shift[i][:], start=False, stop=True)
            sq_own = work.tile([P, picked], BF16, name="sq_own")
            nc.scalar.activation(sq_own[:], neg_edge[i][:], ACT.Square, scale=0.25 if i == 0 else quarter[:, col])
            nc.tensor.matmul(rest[i][:], plus[:], sq_own[:], start=False, stop=False)
            sq_cons = work.tile([P, picked], BF16, name="sq_cons")
            nc.scalar.activation(sq_cons[:], cons_err[:], ACT.Square, scale=1.0 if i == 0 else mask[:, col])
            nc.tensor.matmul(rest[i][:], plus[:], sq_cons[:], start=False, stop=i > 0)

        def parts(i):
            pieces = 2 if i == blocks - 1 else 1
            return [slice(k * picked // pieces, (k + 1) * picked // pieces) for k in range(pieces)]

        def gather(i):
            picked_d.append(work.tile([P, picked], F32, name="picked_d"))
            for part in parts(i):
                looked_up = y_tiles[i][:].indirect(offsets[:, part.start // 16 : part.stop // 16])
                nc.vector.tensor_tensor(picked_d[i][:, part], looked_up, neg_d[i][:, part], ALU.mult)

        def finish(i):
            loss = work.tile([P, picked], F32, name="loss")
            col = slice(i, i + 1)
            if i == 0:
                nc.tensor.matmul(rest[i][:], plus_wide[:], picked_d[i][:], start=False, stop=True)
                nc.scalar.activation(loss[:], rest[i][:], ACT.Identity, bias=log_2[:, col], scale=mask[:, col])
            else:
                for part in parts(i):
                    nc.vector.scalar_tensor_tensor(
                        loss[:, part], rest[i][:, part], log_2[:, col], picked_d[i][:, part], ALU.add, ALU.add
                    )
            for part in parts(i):
                nc.sync.dma_start(out_blocks[:, i, part], loss[:, part])

        for i in range(blocks):
            consistency(i)
            entropy(i)
        for i in range(blocks):
            copy_d(i)
            squares(i)
        for i in range(blocks - 1):
            gather(i)
        for i in range(blocks - 1):
            finish(i)
        gather(blocks - 1)
        finish(blocks - 1)
